import numpy as np
import ml_dtypes


def mxq(x, axis, fmt="e4m3"):
    dtype, down = {"e4m3": (ml_dtypes.float8_e4m3fn, 7), "e5m2": (ml_dtypes.float8_e5m2, 14)}[fmt]
    v = np.moveaxis(np.asarray(x, np.float32).astype(ml_dtypes.bfloat16).astype(np.float64), axis, -1)
    blocks = v.reshape(v.shape[:-1] + (-1, 32))
    amax = np.abs(blocks).max(-1, keepdims=True)
    byte = np.maximum(np.where(amax > 0, np.frexp(amax)[1] - 1 + 127, 0) - down, 1)
    scale = np.exp2(byte - 127.0)
    codes = (blocks / scale).astype(np.float32).astype(dtype).astype(np.float64)
    return np.moveaxis((codes * scale).reshape(v.shape), -1, axis)


WIDE = False


def mx_kscale(k):
    if not WIDE:
        return np.ones(k)
    levels = np.array([10, -10, 5, -5, 0])
    a = np.random.permutation(np.resize(levels, k // 512 * 4)).reshape(k // 512, 4)
    idx = np.arange(k)
    return np.exp2(a[idx // 512, idx % 128 // 32])


BF16 = ml_dtypes.bfloat16


def bf(x):
    return np.asarray(x, np.float32).astype(BF16)


def f64(x):
    return np.asarray(x).astype(np.float64)


B, S, SV, H, DH = 32, 512, 32, 8, 64
SCALE = DH ** (-0.5)


def _flatten_like_module(t):
    b, s, h, dh = t.shape
    return np.transpose(t, (0, 2, 1, 3)).reshape(b, s, h * dh)


def _heads_to_batch(t):
    b, s, d = t.shape
    t = t.reshape(b, s, H, d // H)
    t = np.transpose(t, (0, 2, 1, 3))
    return t.reshape(b * H, s, d // H)


def setup_inputs():
    a = np.sqrt(2.0 / (SCALE * np.sqrt(S)))
    sc = mx_kscale(S)
    f = np.repeat(sc.reshape(H, S // H).T, H, axis=0)[None, :, :, None]
    return {"query": bf(np.random.standard_normal((B, S, H, DH)) * a * f),
            "key": bf(np.random.standard_normal((B, S, H, DH)) * a / f),
            "value": bf(np.random.standard_normal((B, SV, H, DH)))}


def reference(query, key, value):
    q = _heads_to_batch(_flatten_like_module(f64(query)))
    k = _heads_to_batch(_flatten_like_module(f64(key)))
    scores = (mxq(q, 1, "e4m3").transpose(0, 2, 1) @ mxq(k, 1, "e4m3")) * SCALE
    e = np.exp(scores - scores.max(axis=2, keepdims=True))
    return e / e.sum(axis=2, keepdims=True)

@@ -1,0 +1,234 @@
+from contextlib import ExitStack
+
+import concourse.mybir as mybir
+
+FP8X4 = mybir.dt.float8_e4m3fn_x4
+BF16 = mybir.dt.bfloat16
+F32 = mybir.dt.float32
+I32 = mybir.dt.int32
+U32 = mybir.dt.uint32
+U8 = mybir.dt.uint8
+ACT = mybir.ActivationFunctionType
+ALU = mybir.AluOpType
+AX = mybir.AxisListType
+
+P = 128
+B, S, H, DH = 32, 512, 8, 64
+G = 8
+NT = B // 2
+GC = 4
+NC = NT * 2
+ROW = G * H * DH
+GE = H * DH
+CE = GC * GE
+CW = CE // 4
+UNIT = 64
+NU = 2 * GC
+SCALE = DH ** -0.5
+
+FLOPS = 2 * B * G * S * DH * DH
+BYTES = 2 * B * S * H * DH * 2 + B * G * DH * DH * 4
+
+MANUAL = True
+NRAW = 4
+NGRP = 4
+NFIX = 3
+NPS = 6
+LE, LR, LN = 2, 3, 5
+SPLIT_LOADS = 2
+VK = {0: 2, 1: 2}
+SQ = dict((c, 1) for c in range(3, NC, 3))
+
+
+def tile_flaxattention2_t_kernel(tc, query, key, value, out):
+    nc = tc.nc
+    q2 = query.rearrange("b (j g) h d -> (b j) (g h d)", g=G)
+    k2 = key.rearrange("b (j g) h d -> (b j) (g h d)", g=G)
+
+    with ExitStack() as ctx:
+        raw_pool = ctx.enter_context(tc.tile_pool(name="raw", bufs=NRAW))
+        grp_pool = ctx.enter_context(tc.tile_pool(name="grp", bufs=NGRP))
+        fix_pool = ctx.enter_context(tc.tile_pool(name="fix", bufs=1))
+        st_pool = ctx.enter_context(tc.tile_pool(name="st", bufs=6))
+        e_pool = ctx.enter_context(tc.tile_pool(name="e", bufs=4))
+        ps_pool = ctx.enter_context(tc.psum_pool(name="ps", bufs=NPS))
+
+        cw = [fix_pool.tile([P, 2 * CW], U32, name="cw%d" % n, align_bytes=64) for n in range(NFIX)]
+        sc = [fix_pool.tile([P, 2 * CW], U8, name="sc%d" % n, align_bytes=64) for n in range(NFIX)]
+        lq = [fix_pool.tile([P, 2 * CW], U32, name="lq%d" % n, align_bytes=64) for n in range(NFIX)]
+        ls = [fix_pool.tile([P, 2 * CW], U8, name="ls%d" % n, align_bytes=64) for n in range(NFIX)]
+
+        for n in range(NFIX):
+            nc.vector.memset(lq[n][:].bitcast(I32), 0)
+            nc.vector.memset(sc[n][:].bitcast(I32), 0)
+
+        rawq, rawk, grp = {}, {}, {}
+        ps, mx, nmx, sm, rs, et = {}, {}, {}, {}, {}, {}
+
+        def load(i):
+            rawk[i] = raw_pool.tile([P, ROW], BF16, name="rawk")
+            rawq[i] = raw_pool.tile([P, ROW], BF16, name="rawq")
+            cuts = 2 if i < SPLIT_LOADS else 1
+            w = ROW // cuts
+            for a in range(cuts):
+                nc.sync.dma_start(out=rawk[i][:, a * w:(a + 1) * w], in_=k2[i * P:(i + 1) * P, a * w:(a + 1) * w])
+                nc.sync.dma_start(out=rawq[i][:, a * w:(a + 1) * w], in_=q2[i * P:(i + 1) * P, a * w:(a + 1) * w])
+
+        def regroup_v(dst, src, n):
+            nc.vector.tensor_copy(
+                out=dst.rearrange("p (g c i t) -> p g c t i", g=n, c=32, i=4, t=4),
+                in_=src.rearrange("p (g t c i) -> p g c t i", g=n, t=4, c=32, i=4),
+            )
+
+        def regroup_s(dst, src, n):
+            for g in range(n):
+                nc.scalar.copy(
+                    out=dst[:, g * GE:(g + 1) * GE].rearrange("p (c i t) -> p c t i", c=32, i=4, t=4),
+                    in_=src[:, g * GE:(g + 1) * GE].rearrange("p (t c i) -> p c t i", t=4, c=32, i=4),
+                )
+
+        def get_grp(c):
+            if c not in grp:
+                grp[c] = grp_pool.tile([P, 2 * CE], BF16, name="grp", align_bytes=64)
+            return grp[c]
+
+        def regroup(c, op, eng, a, b):
+            raw = (rawq, rawk)[op][c // 2]
+            n_s = SQ.get(c, 0) if op == 0 else GC - VK.get(c, 0)
+            lo, hi = (0, n_s) if eng == "s" else (n_s, GC)
+            lo, hi = max(lo, a), min(hi, b)
+            if hi <= lo:
+                return
+            src = raw[:, (c % 2) * CE + lo * GE:(c % 2) * CE + hi * GE]
+            dst = get_grp(c)[:, op * CE + lo * GE:op * CE + hi * GE]
+            if eng == "s":
+                regroup_s(dst, src, hi - lo)
+            else:
+                regroup_v(dst, src, hi - lo)
+
+        def quant(c):
+            n = c % NFIX
+            nc.vector.quantize_mx(out=cw[n][:].bitcast(FP8X4), scales=sc[n][:], in_=grp[c][:])
+
+        def moves(c):
+            n = c % NFIX
+            src = cw[n][:, 0:CW].bitcast(I32).rearrange("p (u d) -> p u d", u=NU, d=UNIT)
+            dst = lq[n][:].bitcast(I32).rearrange("p (u b d) -> p u b d", u=NU, b=2, d=UNIT)
+            nc.vector.tensor_copy(out=dst[0:64, :, 0, :], in_=src[0:64])
+            nc.vector.tensor_copy(out=dst[64:128, :, 1, :], in_=src[64:128])
+            ssrc = sc[n][:, 0:CW].bitcast(I32).rearrange("p (u w) -> p u w", u=NU, w=UNIT // 4)
+            sdst = ls[n][:].bitcast(I32).rearrange("p (u b w) -> p u b w", u=NU, b=2, w=UNIT // 4)
+            nc.vector.tensor_copy(out=sdst[:, :, 0, :], in_=ssrc)
+            nc.vector.tensor_copy(out=sdst[:, :, 1, :], in_=ssrc)
+
+        def passes(c):
+            n = c % NFIX
+            ps[c] = ps_pool.tile([P, 512], F32, name="ps")
+            for g in range(GC):
+                for hp in range(2):
+                    u = 2 * g + hp
+                    w0 = CW + (u - (g % 2)) * UNIT
+                    nc.tensor.matmul_mx(
+                        out=ps[c][:, g * 128:(g + 1) * 128],
+                        lhsT=lq[n][:, u * 128:(u + 1) * 128].bitcast(FP8X4),
+                        lhsT_scale=ls[n][:, u * 128:(u + 1) * 128],
+                        rhs=cw[n][:, w0:w0 + 128].bitcast(FP8X4),
+                        rhs_scale=sc[n][:, w0:w0 + 128],
+                        start=(hp == 0),
+                        stop=(hp == 1),
+                    )
+
+        def rowmax(c):
+            mx[c] = st_pool.tile([P, GC], F32, name="mx")
+            nc.vector.tensor_reduce(
+                out=mx[c][:].rearrange("p (a b) -> p a b", a=2, b=2),
+                in_=ps[c][:].rearrange("p (a b c) -> p a b c", a=2, b=4, c=64)[:, :, 0:4:3, :],
+                axis=AX.X,
+                op=ALU.max,
+            )
+
+        def negmax(c):
+            nmx[c] = st_pool.tile([P, GC], F32, name="nmx")
+            nc.scalar.mul(out=nmx[c][:], in_=mx[c][:], mul=-SCALE)
+
+        def exps(c):
+            if c % 2 == 0:
+                sm[c // 2] = st_pool.tile([P, G], F32, name="sm")
+                et[c // 2] = e_pool.tile([P, G * DH], F32, name="et")
+            for g in range(GC):
+                off = g * 128 + (g % 2) * 64
+                gg = (c % 2) * GC + g
+                nc.scalar.activation(
+                    out=et[c // 2][:, gg * DH:(gg + 1) * DH],
+                    in_=ps[c][:, off:off + DH],
+                    func=ACT.Exp,
+                    bias=nmx[c][:, g:g + 1],
+                    scale=SCALE,
+                    accum_out=sm[c // 2][:, gg:gg + 1],
+                )
+
+        def recip(i, g0, g1):
+            if i not in rs:
+                rs[i] = st_pool.tile([P, G], F32, name="rs")
+            nc.vector.reciprocal(out=rs[i][:, g0:g1], in_=sm[i][:, g0:g1])
+
+        def norm(c):
+            for g in range(GC):
+                gg = (c % 2) * GC + g
+                nc.scalar.activation(
+                    out=et[c // 2][:, gg * DH:(gg + 1) * DH],
+                    in_=et[c // 2][:, gg * DH:(gg + 1) * DH],
+                    func=ACT.Copy,
+                    scale=rs[c // 2][:, gg:gg + 1],
+                )
+
+        def store(i, g0, g1):
+            for bb in range(2):
+                n0 = (2 * i + bb) * G
+                nc.sync.dma_start(
+                    out=out[n0 + g0:n0 + g1].rearrange("g a c -> a g c"),
+                    in_=et[i][bb * 64:(bb + 1) * 64, g0 * DH:g1 * DH].rearrange("p (g c) -> p g c", g=g1 - g0, c=DH),
+                )
+
+        def ok(c):
+            return 0 <= c < NC
+
+        if MANUAL:
+            ctx.enter_context(tc.manual_schedule())
+
+        for i in range(NRAW):
+            load(i)
+        for c in range(-2, NC + LN + 1):
+            if ok(c):
+                quant(c)
+            if ok(c + 2):
+                regroup(c + 2, 1, "s", 0, 2)
+            if ok(c - LE):
+                negmax(c - LE)
+            e = c - LN
+            if ok(e):
+                norm(e)
+                if e >= NC - 2:
+                    store(e // 2, (e % 2) * GC, (e % 2) * GC + GC)
+                elif e % 2 == 1:
+                    store(e // 2, 0, G)
+            if ok(c - LE):
+                exps(c - LE)
+            if ok(c + 1):
+                regroup(c + 1, 0, "v", 0, GC)
+            if ok(c + 2):
+                regroup(c + 2, 1, "v", 0, GC)
+                regroup(c + 2, 1, "s", 2, GC)
+                regroup(c + 2, 0, "s", 0, GC)
+            if ok(c):
+                moves(c)
+                passes(c)
+            if ok(c - 1):
+                rowmax(c - 1)
+            e = c - LR
+            if ok(e) and e >= NC - 2:
+                recip(e // 2, (e % 2) * GC, (e % 2) * GC + GC)
+            elif ok(e) and e % 2 == 1:
+                recip(e // 2, 0, G)
+            if c >= 0 and c % 2 == 0 and c // 2 + NRAW < NT:
+                load(c // 2 + NRAW)

@@ -36,8 +36,8 @@ NFIX = 3
 NPS = 6
 LE, LR, LN = 2, 3, 5
 SPLIT_LOADS = 2
-VK = {0: 2, 1: 2}
-SQ = dict((c, 1) for c in range(3, NC, 3))
+VK = dict((c, 2 if c < 2 else 1) for c in range(NC))
+SQ = {}
 
 
 def tile_flaxattention2_t_kernel(tc, query, key, value, out):

@@ -16,14 +16,10 @@ P = 128
 B, S, H, DH = 32, 512, 8, 64
 G = 8
 NT = B // 2
-GC = 4
-NC = NT * 2
 ROW = G * H * DH
 GE = H * DH
-CE = GC * GE
-CW = CE // 4
+GW = GE // 4
 UNIT = 64
-NU = 2 * GC
 SCALE = DH ** -0.5
 
 FLOPS = 2 * B * G * S * DH * DH
@@ -31,12 +27,17 @@ BYTES = 2 * B * S * H * DH * 2 + B * G * DH * DH * 4
 
 MANUAL = True
 NRAW = 4
-NGRP = 4
+NGQ = 3
+NGK = 4
 NFIX = 3
-NPS = 6
-LE, LR, LN = 2, 3, 5
+NPS = 8
+LE, LR, LN = 2, 3, 4
+SPLIT_TILES = (0, NT - 1)
 SPLIT_LOADS = 2
-VK = dict((c, 2 if c < 2 else 1) for c in range(NC))
+NM_ON_V = False
+S4D = True
+PLANE1 = True
+VK = {0: 2, 1: 2}
 SQ = {}
 
 
@@ -45,24 +46,36 @@ def tile_flaxattention2_t_kernel(tc, query, key, value, out):
     q2 = query.rearrange("b (j g) h d -> (b j) (g h d)", g=G)
     k2 = key.rearrange("b (j g) h d -> (b j) (g h d)", g=G)
 
+    blocks = []
+    for i in range(NT):
+        if i in SPLIT_TILES:
+            blocks.append((i, 0, 4))
+            blocks.append((i, 4, 8))
+        else:
+            blocks.append((i, 0, 8))
+    nb = len(blocks)
+    last_of_tile = dict((blk[0], n) for n, blk in enumerate(blocks))
+
     with ExitStack() as ctx:
         raw_pool = ctx.enter_context(tc.tile_pool(name="raw", bufs=NRAW))
-        grp_pool = ctx.enter_context(tc.tile_pool(name="grp", bufs=NGRP))
+        grp_pool = ctx.enter_context(tc.tile_pool(name="grp", bufs=1))
         fix_pool = ctx.enter_context(tc.tile_pool(name="fix", bufs=1))
         st_pool = ctx.enter_context(tc.tile_pool(name="st", bufs=6))
         e_pool = ctx.enter_context(tc.tile_pool(name="e", bufs=4))
         ps_pool = ctx.enter_context(tc.psum_pool(name="ps", bufs=NPS))
 
-        cw = [fix_pool.tile([P, 2 * CW], U32, name="cw%d" % n, align_bytes=64) for n in range(NFIX)]
-        sc = [fix_pool.tile([P, 2 * CW], U8, name="sc%d" % n, align_bytes=64) for n in range(NFIX)]
-        lq = [fix_pool.tile([P, 2 * CW], U32, name="lq%d" % n, align_bytes=64) for n in range(NFIX)]
-        ls = [fix_pool.tile([P, 2 * CW], U8, name="ls%d" % n, align_bytes=64) for n in range(NFIX)]
+        cq = [fix_pool.tile([P, G * GW], U32, name="cq%d" % n, align_bytes=64) for n in range(NFIX)]
+        sq = [fix_pool.tile([P, G * GW], U8, name="sq%d" % n, align_bytes=64) for n in range(NFIX)]
+        ck = [fix_pool.tile([P, G * GW], U32, name="ck%d" % n, align_bytes=64) for n in range(NFIX)]
+        sk = [fix_pool.tile([P, G * GW], U8, name="sk%d" % n, align_bytes=64) for n in range(NFIX)]
+        lq = [fix_pool.tile([P, 2 * G * GW], U32, name="lq%d" % n, align_bytes=64) for n in range(NFIX)]
+        ls = [fix_pool.tile([P, 2 * G * GW], U8, name="ls%d" % n, align_bytes=64) for n in range(NFIX)]
 
         for n in range(NFIX):
             nc.vector.memset(lq[n][:].bitcast(I32), 0)
-            nc.vector.memset(sc[n][:].bitcast(I32), 0)
+            nc.vector.memset(sq[n][:].bitcast(I32), 0)
 
-        rawq, rawk, grp = {}, {}, {}
+        rawq, rawk, grpq, grpk = {}, {}, {}, {}
         ps, mx, nmx, sm, rs, et = {}, {}, {}, {}, {}, {}
 
         def load(i):
@@ -74,161 +87,179 @@ def tile_flaxattention2_t_kernel(tc, query, key, value, out):
                 nc.sync.dma_start(out=rawk[i][:, a * w:(a + 1) * w], in_=k2[i * P:(i + 1) * P, a * w:(a + 1) * w])
                 nc.sync.dma_start(out=rawq[i][:, a * w:(a + 1) * w], in_=q2[i * P:(i + 1) * P, a * w:(a + 1) * w])
 
-        def regroup_v(dst, src, n):
-            nc.vector.tensor_copy(
+        def copy4(eng_copy, dst, src, n):
+            eng_copy(
                 out=dst.rearrange("p (g c i t) -> p g c t i", g=n, c=32, i=4, t=4),
                 in_=src.rearrange("p (g t c i) -> p g c t i", g=n, t=4, c=32, i=4),
             )
 
         def regroup_s(dst, src, n):
+            if S4D:
+                copy4(nc.scalar.copy, dst, src, n)
+                return
             for g in range(n):
                 nc.scalar.copy(
                     out=dst[:, g * GE:(g + 1) * GE].rearrange("p (c i t) -> p c t i", c=32, i=4, t=4),
                     in_=src[:, g * GE:(g + 1) * GE].rearrange("p (t c i) -> p c t i", t=4, c=32, i=4),
                 )
 
-        def get_grp(c):
-            if c not in grp:
-                grp[c] = grp_pool.tile([P, 2 * CE], BF16, name="grp", align_bytes=64)
-            return grp[c]
+        def get_grp(b, op):
+            d = (grpq, grpk)[op]
+            if b not in d:
+                d[b] = grp_pool.tile([P, ROW], BF16, name=("grpq", "grpk")[op], align_bytes=64, bufs=(NGQ, NGK)[op])
+            return d[b]
 
-        def regroup(c, op, eng, a, b):
-            raw = (rawq, rawk)[op][c // 2]
-            n_s = SQ.get(c, 0) if op == 0 else GC - VK.get(c, 0)
-            lo, hi = (0, n_s) if eng == "s" else (n_s, GC)
-            lo, hi = max(lo, a), min(hi, b)
+        def regroup(b, op, eng, part, parts):
+            i, g0, g1 = blocks[b]
+            ng = g1 - g0
+            raw = (rawq, rawk)[op][i]
+            n_s = SQ.get(b, 0) if op == 0 else ng - VK.get(b, 0)
+            lo, hi = (0, n_s) if eng == "s" else (n_s, ng)
+            n = hi - lo
+            lo, hi = lo + (n * part) // parts, lo + (n * (part + 1)) // parts
             if hi <= lo:
                 return
-            src = raw[:, (c % 2) * CE + lo * GE:(c % 2) * CE + hi * GE]
-            dst = get_grp(c)[:, op * CE + lo * GE:op * CE + hi * GE]
+            src = raw[:, (g0 + lo) * GE:(g0 + hi) * GE]
+            dst = get_grp(b, op)[:, lo * GE:hi * GE]
             if eng == "s":
                 regroup_s(dst, src, hi - lo)
             else:
-                regroup_v(dst, src, hi - lo)
+                copy4(nc.vector.tensor_copy, dst, src, hi - lo)
 
-        def quant(c):
-            n = c % NFIX
-            nc.vector.quantize_mx(out=cw[n][:].bitcast(FP8X4), scales=sc[n][:], in_=grp[c][:])
+        def quant(b, op):
+            i, g0, g1 = blocks[b]
+            ng = g1 - g0
+            n = b % NFIX
+            codes, scales, grp = ((cq, sq, grpq), (ck, sk, grpk))[op]
+            nc.vector.quantize_mx(
+                out=codes[n][:, 0:ng * GW].bitcast(FP8X4), scales=scales[n][:, 0:ng * GW], in_=grp[b][:, 0:ng * GE]
+            )
 
-        def moves(c):
-            n = c % NFIX
-            src = cw[n][:, 0:CW].bitcast(I32).rearrange("p (u d) -> p u d", u=NU, d=UNIT)
-            dst = lq[n][:].bitcast(I32).rearrange("p (u b d) -> p u b d", u=NU, b=2, d=UNIT)
+        def moves(b):
+            i, g0, g1 = blocks[b]
+            nu = 2 * (g1 - g0)
+            n = b % NFIX
+            src = cq[n][:, 0:nu * UNIT].bitcast(I32).rearrange("p (u d) -> p u d", u=nu, d=UNIT)
+            dst = lq[n][:, 0:2 * nu * UNIT].bitcast(I32).rearrange("p (u b d) -> p u b d", u=nu, b=2, d=UNIT)
             nc.vector.tensor_copy(out=dst[0:64, :, 0, :], in_=src[0:64])
             nc.vector.tensor_copy(out=dst[64:128, :, 1, :], in_=src[64:128])
-            ssrc = sc[n][:, 0:CW].bitcast(I32).rearrange("p (u w) -> p u w", u=NU, w=UNIT // 4)
-            sdst = ls[n][:].bitcast(I32).rearrange("p (u b w) -> p u b w", u=NU, b=2, w=UNIT // 4)
-            nc.vector.tensor_copy(out=sdst[:, :, 0, :], in_=ssrc)
-            nc.vector.tensor_copy(out=sdst[:, :, 1, :], in_=ssrc)
+            ssrc = sq[n][:, 0:nu * UNIT].bitcast(I32).rearrange("p (u w) -> p u w", u=nu, w=UNIT // 4)
+            sdst = ls[n][:, 0:2 * nu * UNIT].bitcast(I32).rearrange("p (u b w) -> p u b w", u=nu, b=2, w=UNIT // 4)
+            if PLANE1:
+                nc.vector.tensor_copy(out=sdst, in_=ssrc.unsqueeze(2).to_broadcast([P, nu, 2, UNIT // 4]))
+            else:
+                nc.vector.tensor_copy(out=sdst[:, :, 0, :], in_=ssrc)
+                nc.vector.tensor_copy(out=sdst[:, :, 1, :], in_=ssrc)
 
-        def passes(c):
-            n = c % NFIX
-            ps[c] = ps_pool.tile([P, 512], F32, name="ps")
-            for g in range(GC):
+        def passes(b):
+            i, g0, g1 = blocks[b]
+            n = b % NFIX
+            ps[b] = [ps_pool.tile([P, 512], F32, name="ps") for k in range((g1 - g0) // 4)]
+            for g in range(g1 - g0):
                 for hp in range(2):
                     u = 2 * g + hp
-                    w0 = CW + (u - (g % 2)) * UNIT
+                    w0 = (u - (g % 2)) * UNIT
                     nc.tensor.matmul_mx(
-                        out=ps[c][:, g * 128:(g + 1) * 128],
+                        out=ps[b][g // 4][:, (g % 4) * 128:(g % 4 + 1) * 128],
                         lhsT=lq[n][:, u * 128:(u + 1) * 128].bitcast(FP8X4),
                         lhsT_scale=ls[n][:, u * 128:(u + 1) * 128],
-                        rhs=cw[n][:, w0:w0 + 128].bitcast(FP8X4),
-                        rhs_scale=sc[n][:, w0:w0 + 128],
+                        rhs=ck[n][:, w0:w0 + 128].bitcast(FP8X4),
+                        rhs_scale=sk[n][:, w0:w0 + 128],
                         start=(hp == 0),
                         stop=(hp == 1),
                     )
 
-        def rowmax(c):
-            mx[c] = st_pool.tile([P, GC], F32, name="mx")
-            nc.vector.tensor_reduce(
-                out=mx[c][:].rearrange("p (a b) -> p a b", a=2, b=2),
-                in_=ps[c][:].rearrange("p (a b c) -> p a b c", a=2, b=4, c=64)[:, :, 0:4:3, :],
-                axis=AX.X,
-                op=ALU.max,
-            )
+        def rowmax(b):
+            mx[b] = st_pool.tile([P, G], F32, name="mx")
+            for k in range(len(ps[b])):
+                nc.vector.tensor_reduce(
+                    out=mx[b][:, k * 4:(k + 1) * 4].rearrange("p (a b) -> p a b", a=2, b=2),
+                    in_=ps[b][k][:].rearrange("p (a b c) -> p a b c", a=2, b=4, c=64)[:, :, 0:4:3, :],
+                    axis=AX.X,
+                    op=ALU.max,
+                )
 
-        def negmax(c):
-            nmx[c] = st_pool.tile([P, GC], F32, name="nmx")
-            nc.scalar.mul(out=nmx[c][:], in_=mx[c][:], mul=-SCALE)
+        def negmax(b):
+            ng = blocks[b][2] - blocks[b][1]
+            nmx[b] = st_pool.tile([P, G], F32, name="nmx")
+            nc.scalar.mul(out=nmx[b][:, 0:ng], in_=mx[b][:, 0:ng], mul=-SCALE)
 
-        def exps(c):
-            if c % 2 == 0:
-                sm[c // 2] = st_pool.tile([P, G], F32, name="sm")
-                et[c // 2] = e_pool.tile([P, G * DH], F32, name="et")
-            for g in range(GC):
-                off = g * 128 + (g % 2) * 64
-                gg = (c % 2) * GC + g
+        def exps(b):
+            ng = blocks[b][2] - blocks[b][1]
+            sm[b] = st_pool.tile([P, G], F32, name="sm")
+            et[b] = e_pool.tile([P, G * DH], F32, name="et")
+            for g in range(ng):
+                off = (g % 4) * 128 + (g % 2) * 64
                 nc.scalar.activation(
-                    out=et[c // 2][:, gg * DH:(gg + 1) * DH],
-                    in_=ps[c][:, off:off + DH],
+                    out=et[b][:, g * DH:(g + 1) * DH],
+                    in_=ps[b][g // 4][:, off:off + DH],
                     func=ACT.Exp,
-                    bias=nmx[c][:, g:g + 1],
+                    bias=nmx[b][:, g:g + 1],
                     scale=SCALE,
-                    accum_out=sm[c // 2][:, gg:gg + 1],
+                    accum_out=sm[b][:, g:g + 1],
                 )
 
-        def recip(i, g0, g1):
-            if i not in rs:
-                rs[i] = st_pool.tile([P, G], F32, name="rs")
-            nc.vector.reciprocal(out=rs[i][:, g0:g1], in_=sm[i][:, g0:g1])
+        def recip(b):
+            ng = blocks[b][2] - blocks[b][1]
+            rs[b] = st_pool.tile([P, G], F32, name="rs")
+            nc.vector.reciprocal(out=rs[b][:, 0:ng], in_=sm[b][:, 0:ng])
 
-        def norm(c):
-            for g in range(GC):
-                gg = (c % 2) * GC + g
-                nc.scalar.activation(
-                    out=et[c // 2][:, gg * DH:(gg + 1) * DH],
-                    in_=et[c // 2][:, gg * DH:(gg + 1) * DH],
-                    func=ACT.Copy,
-                    scale=rs[c // 2][:, gg:gg + 1],
+        def norm_store(b):
+            i, g0, g1 = blocks[b]
+            ng = g1 - g0
+            if NM_ON_V:
+                v = et[b][:, 0:ng * DH].rearrange("p (g c) -> p g c", g=ng, c=DH)
+                nc.vector.tensor_tensor(
+                    out=v, in0=v, in1=rs[b][:, 0:ng].unsqueeze(2).to_broadcast([P, ng, DH]), op=ALU.mult
                 )
-
-        def store(i, g0, g1):
+            else:
+                for g in range(ng):
+                    nc.scalar.activation(
+                        out=et[b][:, g * DH:(g + 1) * DH],
+                        in_=et[b][:, g * DH:(g + 1) * DH],
+                        func=ACT.Copy,
+                        scale=rs[b][:, g:g + 1],
+                    )
             for bb in range(2):
                 n0 = (2 * i + bb) * G
                 nc.sync.dma_start(
                     out=out[n0 + g0:n0 + g1].rearrange("g a c -> a g c"),
-                    in_=et[i][bb * 64:(bb + 1) * 64, g0 * DH:g1 * DH].rearrange("p (g c) -> p g c", g=g1 - g0, c=DH),
+                    in_=et[b][bb * 64:(bb + 1) * 64, 0:ng * DH].rearrange("p (g c) -> p g c", g=ng, c=DH),
                 )
 
-        def ok(c):
-            return 0 <= c < NC
+        def ok(b):
+            return 0 <= b < nb
 
         if MANUAL:
             ctx.enter_context(tc.manual_schedule())
 
         for i in range(NRAW):
             load(i)
-        for c in range(-2, NC + LN + 1):
-            if ok(c):
-                quant(c)
-            if ok(c + 2):
-                regroup(c + 2, 1, "s", 0, 2)
-            if ok(c - LE):
-                negmax(c - LE)
-            e = c - LN
-            if ok(e):
-                norm(e)
-                if e >= NC - 2:
-                    store(e // 2, (e % 2) * GC, (e % 2) * GC + GC)
-                elif e % 2 == 1:
-                    store(e // 2, 0, G)
-            if ok(c - LE):
-                exps(c - LE)
-            if ok(c + 1):
-                regroup(c + 1, 0, "v", 0, GC)
-            if ok(c + 2):
-                regroup(c + 2, 1, "v", 0, GC)
-                regroup(c + 2, 1, "s", 2, GC)
-                regroup(c + 2, 0, "s", 0, GC)
-            if ok(c):
-                moves(c)
-                passes(c)
-            if ok(c - 1):
-                rowmax(c - 1)
-            e = c - LR
-            if ok(e) and e >= NC - 2:
-                recip(e // 2, (e % 2) * GC, (e % 2) * GC + GC)
-            elif ok(e) and e % 2 == 1:
-                recip(e // 2, 0, G)
-            if c >= 0 and c % 2 == 0 and c // 2 + NRAW < NT:
-                load(c // 2 + NRAW)
+        for it in range(-2, nb + LN + 1):
+            if ok(it):
+                quant(it, 0)
+            if ok(it + 2):
+                regroup(it + 2, 1, "s", 0, 2)
+            if ok(it - LE):
+                negmax(it - LE)
+            if ok(it - LN):
+                norm_store(it - LN)
+            if ok(it - LE):
+                exps(it - LE)
+            if ok(it):
+                quant(it, 1)
+            if ok(it + 1):
+                regroup(it + 1, 0, "v", 0, 1)
+            if ok(it + 2):
+                regroup(it + 2, 1, "v", 0, 1)
+                regroup(it + 2, 1, "s", 1, 2)
+                regroup(it + 2, 0, "s", 0, 1)
+            if ok(it):
+                moves(it)
+                passes(it)
+            if ok(it - 1):
+                rowmax(it - 1)
+            if ok(it - LR):
+                recip(it - LR)
+            if ok(it + 1) and last_of_tile[blocks[it + 1][0]] == it + 1 and blocks[it + 1][0] + NRAW < NT:
+                load(blocks[it + 1][0] + NRAW)

@@ -34,10 +34,11 @@ NPS = 8
 LE, LR, LN = 2, 3, 4
 SPLIT_TILES = (0, NT - 1)
 SPLIT_LOADS = 2
-NM_ON_V = False
+NM_V_LAST = 4
+RG_PARTS = 1
 S4D = True
 PLANE1 = True
-VK = {0: 2, 1: 2}
+VK = {}
 SQ = {}
 
 
@@ -207,7 +208,7 @@ def tile_flaxattention2_t_kernel(tc, query, key, value, out):
         def norm_store(b):
             i, g0, g1 = blocks[b]
             ng = g1 - g0
-            if NM_ON_V:
+            if b >= nb - NM_V_LAST:
                 v = et[b][:, 0:ng * DH].rearrange("p (g c) -> p g c", g=ng, c=DH)
                 nc.vector.tensor_tensor(
                     out=v, in0=v, in1=rs[b][:, 0:ng].unsqueeze(2).to_broadcast([P, ng, DH]), op=ALU.mult
@@ -239,7 +240,7 @@ def tile_flaxattention2_t_kernel(tc, query, key, value, out):
             if ok(it):
                 quant(it, 0)
             if ok(it + 2):
-                regroup(it + 2, 1, "s", 0, 2)
+                regroup(it + 2, 1, "s", 0, RG_PARTS)
             if ok(it - LE):
                 negmax(it - LE)
             if ok(it - LN):
@@ -252,7 +253,8 @@ def tile_flaxattention2_t_kernel(tc, query, key, value, out):
                 regroup(it + 1, 0, "v", 0, 1)
             if ok(it + 2):
                 regroup(it + 2, 1, "v", 0, 1)
-                regroup(it + 2, 1, "s", 1, 2)
+                if RG_PARTS == 2:
+                    regroup(it + 2, 1, "s", 1, 2)
                 regroup(it + 2, 0, "s", 0, 1)
             if ok(it):
                 moves(it)

@@ -37,7 +37,8 @@ SPLIT_LOADS = 2
 NM_V_LAST = 4
 RG_PARTS = 1
 S4D = True
-PLANE1 = True
+PLANE_DMA = False
+BOT_DMA = tuple(range(3, 16))
 VK = {}
 SQ = {}
 
@@ -75,6 +76,8 @@ def tile_flaxattention2_t_kernel(tc, query, key, value, out):
         for n in range(NFIX):
             nc.vector.memset(lq[n][:].bitcast(I32), 0)
             nc.vector.memset(sq[n][:].bitcast(I32), 0)
+            if PLANE_DMA:
+                nc.vector.memset(ls[n][:].bitcast(I32), 0)
 
         rawq, rawk, grpq, grpk = {}, {}, {}, {}
         ps, mx, nmx, sm, rs, et = {}, {}, {}, {}, {}, {}
@@ -136,21 +139,31 @@ def tile_flaxattention2_t_kernel(tc, query, key, value, out):
                 out=codes[n][:, 0:ng * GW].bitcast(FP8X4), scales=scales[n][:, 0:ng * GW], in_=grp[b][:, 0:ng * GE]
             )
 
-        def moves(b):
+        def views(b):
             i, g0, g1 = blocks[b]
             nu = 2 * (g1 - g0)
             n = b % NFIX
             src = cq[n][:, 0:nu * UNIT].bitcast(I32).rearrange("p (u d) -> p u d", u=nu, d=UNIT)
             dst = lq[n][:, 0:2 * nu * UNIT].bitcast(I32).rearrange("p (u b d) -> p u b d", u=nu, b=2, d=UNIT)
-            nc.vector.tensor_copy(out=dst[0:64, :, 0, :], in_=src[0:64])
-            nc.vector.tensor_copy(out=dst[64:128, :, 1, :], in_=src[64:128])
             ssrc = sq[n][:, 0:nu * UNIT].bitcast(I32).rearrange("p (u w) -> p u w", u=nu, w=UNIT // 4)
             sdst = ls[n][:, 0:2 * nu * UNIT].bitcast(I32).rearrange("p (u b w) -> p u b w", u=nu, b=2, w=UNIT // 4)
-            if PLANE1:
+            return nu, src, dst, ssrc, sdst
+
+        def dma_moves(b):
+            nu, src, dst, ssrc, sdst = views(b)
+            if PLANE_DMA:
+                nc.sync.dma_start(out=sdst[0:64, :, 0, :], in_=ssrc[0:64])
+                nc.sync.dma_start(out=sdst[64:128, :, 1, :], in_=ssrc[64:128])
+            if b in BOT_DMA:
+                nc.sync.dma_start(out=dst[64:128, :, 1, :], in_=src[64:128])
+
+        def moves(b):
+            nu, src, dst, ssrc, sdst = views(b)
+            nc.vector.tensor_copy(out=dst[0:64, :, 0, :], in_=src[0:64])
+            if b not in BOT_DMA:
+                nc.vector.tensor_copy(out=dst[64:128, :, 1, :], in_=src[64:128])
+            if not PLANE_DMA:
                 nc.vector.tensor_copy(out=sdst, in_=ssrc.unsqueeze(2).to_broadcast([P, nu, 2, UNIT // 4]))
-            else:
-                nc.vector.tensor_copy(out=sdst[:, :, 0, :], in_=ssrc)
-                nc.vector.tensor_copy(out=sdst[:, :, 1, :], in_=ssrc)
 
         def passes(b):
             i, g0, g1 = blocks[b]
@@ -239,6 +252,7 @@ def tile_flaxattention2_t_kernel(tc, query, key, value, out):
         for it in range(-2, nb + LN + 1):
             if ok(it):
                 quant(it, 0)
+                dma_moves(it)
             if ok(it + 2):
                 regroup(it + 2, 1, "s", 0, RG_PARTS)
             if ok(it - LE):

@@ -25,22 +25,17 @@ SCALE = DH ** -0.5
 FLOPS = 2 * B * G * S * DH * DH
 BYTES = 2 * B * S * H * DH * 2 + B * G * DH * DH * 4
 
-MANUAL = True
 NRAW = 4
 NGQ = 3
 NGK = 4
-NFIX = 3
+NPAIR = 2
+NK = 4
 NPS = 8
-LE, LR, LN = 2, 3, 4
+LM, LE, LR, LN = 2, 3, 4, 5
 SPLIT_TILES = (0, NT - 1)
 SPLIT_LOADS = 2
-NM_V_LAST = 4
-RG_PARTS = 1
-S4D = True
-PLANE_DMA = False
-BOT_DMA = tuple(range(3, 16))
+NM_V_LAST = 6
 VK = {}
-SQ = {}
 
 
 def tile_flaxattention2_t_kernel(tc, query, key, value, out):
@@ -58,26 +53,31 @@ def tile_flaxattention2_t_kernel(tc, query, key, value, out):
     nb = len(blocks)
     last_of_tile = dict((blk[0], n) for n, blk in enumerate(blocks))
 
+    def size(b):
+        return blocks[b][2] - blocks[b][1]
+
+    def goff(b):
+        return size(b - 1) if b % 2 == 1 else 0
+
     with ExitStack() as ctx:
         raw_pool = ctx.enter_context(tc.tile_pool(name="raw", bufs=NRAW))
         grp_pool = ctx.enter_context(tc.tile_pool(name="grp", bufs=1))
         fix_pool = ctx.enter_context(tc.tile_pool(name="fix", bufs=1))
-        st_pool = ctx.enter_context(tc.tile_pool(name="st", bufs=6))
-        e_pool = ctx.enter_context(tc.tile_pool(name="e", bufs=4))
+        st_pool = ctx.enter_context(tc.tile_pool(name="st", bufs=7))
+        e_pool = ctx.enter_context(tc.tile_pool(name="e", bufs=5))
         ps_pool = ctx.enter_context(tc.psum_pool(name="ps", bufs=NPS))
 
-        cq = [fix_pool.tile([P, G * GW], U32, name="cq%d" % n, align_bytes=64) for n in range(NFIX)]
-        sq = [fix_pool.tile([P, G * GW], U8, name="sq%d" % n, align_bytes=64) for n in range(NFIX)]
-        ck = [fix_pool.tile([P, G * GW], U32, name="ck%d" % n, align_bytes=64) for n in range(NFIX)]
-        sk = [fix_pool.tile([P, G * GW], U8, name="sk%d" % n, align_bytes=64) for n in range(NFIX)]
-        lq = [fix_pool.tile([P, 2 * G * GW], U32, name="lq%d" % n, align_bytes=64) for n in range(NFIX)]
-        ls = [fix_pool.tile([P, 2 * G * GW], U8, name="ls%d" % n, align_bytes=64) for n in range(NFIX)]
+        cq = [fix_pool.tile([P, 2 * G * GW], U32, name="cq%d" % n, align_bytes=64) for n in range(NPAIR)]
+        sq = [fix_pool.tile([P, 2 * G * GW], U8, name="sq%d" % n, align_bytes=64) for n in range(NPAIR)]
+        lq = [fix_pool.tile([P, 4 * G * GW], U32, name="lq%d" % n, align_bytes=64) for n in range(NPAIR)]
+        ls = [fix_pool.tile([P, 4 * G * GW], U8, name="ls%d" % n, align_bytes=64) for n in range(NPAIR)]
+        ck = [fix_pool.tile([P, G * GW], U32, name="ck%d" % n, align_bytes=64) for n in range(NK)]
+        sk = [fix_pool.tile([P, G * GW], U8, name="sk%d" % n, align_bytes=64) for n in range(NK)]
 
-        for n in range(NFIX):
-            nc.vector.memset(lq[n][:].bitcast(I32), 0)
-            nc.vector.memset(sq[n][:].bitcast(I32), 0)
-            if PLANE_DMA:
-                nc.vector.memset(ls[n][:].bitcast(I32), 0)
+        half = 2 * G * GW
+
+        def zero(n, a):
+            nc.vector.memset(lq[n][:, a * half:(a + 1) * half].bitcast(I32), 0)
 
         rawq, rawk, grpq, grpk = {}, {}, {}, {}
         ps, mx, nmx, sm, rs, et = {}, {}, {}, {}, {}, {}
@@ -91,94 +91,65 @@ def tile_flaxattention2_t_kernel(tc, query, key, value, out):
                 nc.sync.dma_start(out=rawk[i][:, a * w:(a + 1) * w], in_=k2[i * P:(i + 1) * P, a * w:(a + 1) * w])
                 nc.sync.dma_start(out=rawq[i][:, a * w:(a + 1) * w], in_=q2[i * P:(i + 1) * P, a * w:(a + 1) * w])
 
-        def copy4(eng_copy, dst, src, n):
-            eng_copy(
-                out=dst.rearrange("p (g c i t) -> p g c t i", g=n, c=32, i=4, t=4),
-                in_=src.rearrange("p (g t c i) -> p g c t i", g=n, t=4, c=32, i=4),
-            )
-
-        def regroup_s(dst, src, n):
-            if S4D:
-                copy4(nc.scalar.copy, dst, src, n)
-                return
-            for g in range(n):
-                nc.scalar.copy(
-                    out=dst[:, g * GE:(g + 1) * GE].rearrange("p (c i t) -> p c t i", c=32, i=4, t=4),
-                    in_=src[:, g * GE:(g + 1) * GE].rearrange("p (t c i) -> p c t i", t=4, c=32, i=4),
-                )
-
         def get_grp(b, op):
             d = (grpq, grpk)[op]
             if b not in d:
                 d[b] = grp_pool.tile([P, ROW], BF16, name=("grpq", "grpk")[op], align_bytes=64, bufs=(NGQ, NGK)[op])
             return d[b]
 
-        def regroup(b, op, eng, part, parts):
+        def regroup(b, op, eng):
             i, g0, g1 = blocks[b]
             ng = g1 - g0
             raw = (rawq, rawk)[op][i]
-            n_s = SQ.get(b, 0) if op == 0 else ng - VK.get(b, 0)
+            n_s = 0 if op == 0 else ng - VK.get(b, 0)
             lo, hi = (0, n_s) if eng == "s" else (n_s, ng)
-            n = hi - lo
-            lo, hi = lo + (n * part) // parts, lo + (n * (part + 1)) // parts
             if hi <= lo:
                 return
-            src = raw[:, (g0 + lo) * GE:(g0 + hi) * GE]
-            dst = get_grp(b, op)[:, lo * GE:hi * GE]
-            if eng == "s":
-                regroup_s(dst, src, hi - lo)
-            else:
-                copy4(nc.vector.tensor_copy, dst, src, hi - lo)
-
-        def quant(b, op):
-            i, g0, g1 = blocks[b]
-            ng = g1 - g0
-            n = b % NFIX
-            codes, scales, grp = ((cq, sq, grpq), (ck, sk, grpk))[op]
-            nc.vector.quantize_mx(
-                out=codes[n][:, 0:ng * GW].bitcast(FP8X4), scales=scales[n][:, 0:ng * GW], in_=grp[b][:, 0:ng * GE]
+            n = hi - lo
+            copy = nc.scalar.copy if eng == "s" else nc.vector.tensor_copy
+            copy(
+                out=get_grp(b, op)[:, lo * GE:hi * GE].rearrange("p (g c i t) -> p g c t i", g=n, c=32, i=4, t=4),
+                in_=raw[:, (g0 + lo) * GE:(g0 + hi) * GE].rearrange("p (g t c i) -> p g c t i", g=n, t=4, c=32, i=4),
             )
 
-        def views(b):
-            i, g0, g1 = blocks[b]
-            nu = 2 * (g1 - g0)
-            n = b % NFIX
+        def quant(b, op):
+            ng = size(b)
+            if op == 0:
+                codes, scales, grp, a = cq[(b // 2) % NPAIR], sq[(b // 2) % NPAIR], grpq, goff(b)
+            else:
+                codes, scales, grp, a = ck[b % NK], sk[b % NK], grpk, 0
+            nc.vector.quantize_mx(
+                out=codes[:, a * GW:(a + ng) * GW].bitcast(FP8X4),
+                scales=scales[:, a * GW:(a + ng) * GW],
+                in_=grp[b][:, 0:ng * GE],
+            )
+
+        def moves(pr):
+            nu = 2 * (size(2 * pr) + size(2 * pr + 1))
+            n = pr % NPAIR
             src = cq[n][:, 0:nu * UNIT].bitcast(I32).rearrange("p (u d) -> p u d", u=nu, d=UNIT)
             dst = lq[n][:, 0:2 * nu * UNIT].bitcast(I32).rearrange("p (u b d) -> p u b d", u=nu, b=2, d=UNIT)
             ssrc = sq[n][:, 0:nu * UNIT].bitcast(I32).rearrange("p (u w) -> p u w", u=nu, w=UNIT // 4)
             sdst = ls[n][:, 0:2 * nu * UNIT].bitcast(I32).rearrange("p (u b w) -> p u b w", u=nu, b=2, w=UNIT // 4)
-            return nu, src, dst, ssrc, sdst
-
-        def dma_moves(b):
-            nu, src, dst, ssrc, sdst = views(b)
-            if PLANE_DMA:
-                nc.sync.dma_start(out=sdst[0:64, :, 0, :], in_=ssrc[0:64])
-                nc.sync.dma_start(out=sdst[64:128, :, 1, :], in_=ssrc[64:128])
-            if b in BOT_DMA:
-                nc.sync.dma_start(out=dst[64:128, :, 1, :], in_=src[64:128])
-
-        def moves(b):
-            nu, src, dst, ssrc, sdst = views(b)
+            nc.vector.tensor_copy(out=sdst, in_=ssrc.unsqueeze(2).to_broadcast([P, nu, 2, UNIT // 4]))
             nc.vector.tensor_copy(out=dst[0:64, :, 0, :], in_=src[0:64])
-            if b not in BOT_DMA:
-                nc.vector.tensor_copy(out=dst[64:128, :, 1, :], in_=src[64:128])
-            if not PLANE_DMA:
-                nc.vector.tensor_copy(out=sdst, in_=ssrc.unsqueeze(2).to_broadcast([P, nu, 2, UNIT // 4]))
+            nc.vector.tensor_copy(out=dst[64:128, :, 1, :], in_=src[64:128])
 
         def passes(b):
-            i, g0, g1 = blocks[b]
-            n = b % NFIX
-            ps[b] = [ps_pool.tile([P, 512], F32, name="ps") for k in range((g1 - g0) // 4)]
-            for g in range(g1 - g0):
+            n = (b // 2) % NPAIR
+            m = b % NK
+            ps[b] = [ps_pool.tile([P, 512], F32, name="ps") for k in range(size(b) // 4)]
+            for g in range(size(b)):
                 for hp in range(2):
                     u = 2 * g + hp
                     w0 = (u - (g % 2)) * UNIT
+                    v = 2 * goff(b) + u
                     nc.tensor.matmul_mx(
                         out=ps[b][g // 4][:, (g % 4) * 128:(g % 4 + 1) * 128],
-                        lhsT=lq[n][:, u * 128:(u + 1) * 128].bitcast(FP8X4),
-                        lhsT_scale=ls[n][:, u * 128:(u + 1) * 128],
-                        rhs=ck[n][:, w0:w0 + 128].bitcast(FP8X4),
-                        rhs_scale=sk[n][:, w0:w0 + 128],
+                        lhsT=lq[n][:, v * 128:(v + 1) * 128].bitcast(FP8X4),
+                        lhsT_scale=ls[n][:, v * 128:(v + 1) * 128],
+                        rhs=ck[m][:, w0:w0 + 128].bitcast(FP8X4),
+                        rhs_scale=sk[m][:, w0:w0 + 128],
                         start=(hp == 0),
                         stop=(hp == 1),
                     )
@@ -194,15 +165,14 @@ def tile_flaxattention2_t_kernel(tc, query, key, value, out):
                 )
 
         def negmax(b):
-            ng = blocks[b][2] - blocks[b][1]
+            ng = size(b)
             nmx[b] = st_pool.tile([P, G], F32, name="nmx")
             nc.scalar.mul(out=nmx[b][:, 0:ng], in_=mx[b][:, 0:ng], mul=-SCALE)
 
         def exps(b):
-            ng = blocks[b][2] - blocks[b][1]
             sm[b] = st_pool.tile([P, G], F32, name="sm")
             et[b] = e_pool.tile([P, G * DH], F32, name="et")
-            for g in range(ng):
+            for g in range(size(b)):
                 off = (g % 4) * 128 + (g % 2) * 64
                 nc.scalar.activation(
                     out=et[b][:, g * DH:(g + 1) * DH],
@@ -214,7 +184,7 @@ def tile_flaxattention2_t_kernel(tc, query, key, value, out):
                 )
 
         def recip(b):
-            ng = blocks[b][2] - blocks[b][1]
+            ng = size(b)
             rs[b] = st_pool.tile([P, G], F32, name="rs")
             nc.vector.reciprocal(out=rs[b][:, 0:ng], in_=sm[b][:, 0:ng])
 
@@ -244,17 +214,19 @@ def tile_flaxattention2_t_kernel(tc, query, key, value, out):
         def ok(b):
             return 0 <= b < nb
 
-        if MANUAL:
-            ctx.enter_context(tc.manual_schedule())
+        ctx.enter_context(tc.manual_schedule())
 
+        zero(0, 0)
+        for n in range(NPAIR):
+            nc.vector.memset(sq[n][:].bitcast(I32), 0)
+        zero(1, 0)
         for i in range(NRAW):
             load(i)
         for it in range(-2, nb + LN + 1):
             if ok(it):
                 quant(it, 0)
-                dma_moves(it)
             if ok(it + 2):
-                regroup(it + 2, 1, "s", 0, RG_PARTS)
+                regroup(it + 2, 1, "s")
             if ok(it - LE):
                 negmax(it - LE)
             if ok(it - LN):
@@ -264,17 +236,19 @@ def tile_flaxattention2_t_kernel(tc, query, key, value, out):
             if ok(it):
                 quant(it, 1)
             if ok(it + 1):
-                regroup(it + 1, 0, "v", 0, 1)
+                regroup(it + 1, 0, "v")
             if ok(it + 2):
-                regroup(it + 2, 1, "v", 0, 1)
-                if RG_PARTS == 2:
-                    regroup(it + 2, 1, "s", 1, 2)
-                regroup(it + 2, 0, "s", 0, 1)
-            if ok(it):
-                moves(it)
+                regroup(it + 2, 1, "v")
+            if it == -1:
+                zero(1, 1)
+            if it == 0:
+                zero(0, 1)
+            if ok(it) and it % 2 == 1:
+                moves(it // 2)
+                passes(it - 1)
                 passes(it)
-            if ok(it - 1):
-                rowmax(it - 1)
+            if ok(it - LM):
+                rowmax(it - LM)
             if ok(it - LR):
                 recip(it - LR)
             if ok(it + 1) and last_of_tile[blocks[it + 1][0]] == it + 1 and blocks[it + 1][0] + NRAW < NT:

from contextlib import ExitStack

import concourse.mybir as mybir

FP8X4 = mybir.dt.float8_e4m3fn_x4
BF16 = mybir.dt.bfloat16
F32 = mybir.dt.float32
I32 = mybir.dt.int32
U32 = mybir.dt.uint32
U8 = mybir.dt.uint8
ACT = mybir.ActivationFunctionType
ALU = mybir.AluOpType
AX = mybir.AxisListType

P = 128
B, S, H, DH = 32, 512, 8, 64
G = 8
NT = B // 2
ROW = G * H * DH
GE = H * DH
GW = GE // 4
UNIT = 64
SCALE = DH ** -0.5

FLOPS = 2 * B * G * S * DH * DH
BYTES = 2 * B * S * H * DH * 2 + B * G * DH * DH * 4

NRAW = 4
NGQ = 3
NGK = 4
NPAIR = 2
NK = 4
NPS = 8
LM, LE, LR, LN = 2, 3, 4, 5
SPLIT_TILES = (0, NT - 1)
SPLIT_LOADS = 2
NM_V_LAST = 6
VK = {}


def tile_flaxattention2_t_kernel(tc, query, key, value, out):
    nc = tc.nc
    q2 = query.rearrange("b (j g) h d -> (b j) (g h d)", g=G)
    k2 = key.rearrange("b (j g) h d -> (b j) (g h d)", g=G)

    blocks = []
    for i in range(NT):
        if i in SPLIT_TILES:
            blocks.append((i, 0, 4))
            blocks.append((i, 4, 8))
        else:
            blocks.append((i, 0, 8))
    nb = len(blocks)
    last_of_tile = dict((blk[0], n) for n, blk in enumerate(blocks))

    def size(b):
        return blocks[b][2] - blocks[b][1]

    def goff(b):
        return size(b - 1) if b % 2 == 1 else 0

    with ExitStack() as ctx:
        raw_pool = ctx.enter_context(tc.tile_pool(name="raw", bufs=NRAW))
        grp_pool = ctx.enter_context(tc.tile_pool(name="grp", bufs=1))
        fix_pool = ctx.enter_context(tc.tile_pool(name="fix", bufs=1))
        st_pool = ctx.enter_context(tc.tile_pool(name="st", bufs=7))
        e_pool = ctx.enter_context(tc.tile_pool(name="e", bufs=5))
        ps_pool = ctx.enter_context(tc.psum_pool(name="ps", bufs=NPS))

        cq = [fix_pool.tile([P, 2 * G * GW], U32, name="cq%d" % n, align_bytes=64) for n in range(NPAIR)]
        sq = [fix_pool.tile([P, 2 * G * GW], U8, name="sq%d" % n, align_bytes=64) for n in range(NPAIR)]
        lq = [fix_pool.tile([P, 4 * G * GW], U32, name="lq%d" % n, align_bytes=64) for n in range(NPAIR)]
        ls = [fix_pool.tile([P, 4 * G * GW], U8, name="ls%d" % n, align_bytes=64) for n in range(NPAIR)]
        ck = [fix_pool.tile([P, G * GW], U32, name="ck%d" % n, align_bytes=64) for n in range(NK)]
        sk = [fix_pool.tile([P, G * GW], U8, name="sk%d" % n, align_bytes=64) for n in range(NK)]

        half = 2 * G * GW

        def zero(n, a):
            nc.vector.memset(lq[n][:, a * half:(a + 1) * half].bitcast(I32), 0)

        rawq, rawk, grpq, grpk = {}, {}, {}, {}
        ps, mx, nmx, sm, rs, et = {}, {}, {}, {}, {}, {}

        def load(i):
            rawk[i] = raw_pool.tile([P, ROW], BF16, name="rawk")
            rawq[i] = raw_pool.tile([P, ROW], BF16, name="rawq")
            cuts = 2 if i < SPLIT_LOADS else 1
            w = ROW // cuts
            for a in range(cuts):
                nc.sync.dma_start(out=rawk[i][:, a * w:(a + 1) * w], in_=k2[i * P:(i + 1) * P, a * w:(a + 1) * w])
                nc.sync.dma_start(out=rawq[i][:, a * w:(a + 1) * w], in_=q2[i * P:(i + 1) * P, a * w:(a + 1) * w])

        def get_grp(b, op):
            d = (grpq, grpk)[op]
            if b not in d:
                d[b] = grp_pool.tile([P, ROW], BF16, name=("grpq", "grpk")[op], align_bytes=64, bufs=(NGQ, NGK)[op])
            return d[b]

        def regroup(b, op, eng):
            i, g0, g1 = blocks[b]
            ng = g1 - g0
            raw = (rawq, rawk)[op][i]
            n_s = 0 if op == 0 else ng - VK.get(b, 0)
            lo, hi = (0, n_s) if eng == "s" else (n_s, ng)
            if hi <= lo:
                return
            n = hi - lo
            copy = nc.scalar.copy if eng == "s" else nc.vector.tensor_copy
            copy(
                out=get_grp(b, op)[:, lo * GE:hi * GE].rearrange("p (g c i t) -> p g c t i", g=n, c=32, i=4, t=4),
                in_=raw[:, (g0 + lo) * GE:(g0 + hi) * GE].rearrange("p (g t c i) -> p g c t i", g=n, t=4, c=32, i=4),
            )

        def quant(b, op):
            ng = size(b)
            if op == 0:
                codes, scales, grp, a = cq[(b // 2) % NPAIR], sq[(b // 2) % NPAIR], grpq, goff(b)
            else:
                codes, scales, grp, a = ck[b % NK], sk[b % NK], grpk, 0
            nc.vector.quantize_mx(
                out=codes[:, a * GW:(a + ng) * GW].bitcast(FP8X4),
                scales=scales[:, a * GW:(a + ng) * GW],
                in_=grp[b][:, 0:ng * GE],
            )

        def moves(pr):
            nu = 2 * (size(2 * pr) + size(2 * pr + 1))
            n = pr % NPAIR
            src = cq[n][:, 0:nu * UNIT].bitcast(I32).rearrange("p (u d) -> p u d", u=nu, d=UNIT)
            dst = lq[n][:, 0:2 * nu * UNIT].bitcast(I32).rearrange("p (u b d) -> p u b d", u=nu, b=2, d=UNIT)
            ssrc = sq[n][:, 0:nu * UNIT].bitcast(I32).rearrange("p (u w) -> p u w", u=nu, w=UNIT // 4)
            sdst = ls[n][:, 0:2 * nu * UNIT].bitcast(I32).rearrange("p (u b w) -> p u b w", u=nu, b=2, w=UNIT // 4)
            nc.vector.tensor_copy(out=sdst, in_=ssrc.unsqueeze(2).to_broadcast([P, nu, 2, UNIT // 4]))
            nc.vector.tensor_copy(out=dst[0:64, :, 0, :], in_=src[0:64])
            nc.vector.tensor_copy(out=dst[64:128, :, 1, :], in_=src[64:128])

        def passes(b):
            n = (b // 2) % NPAIR
            m = b % NK
            ps[b] = [ps_pool.tile([P, 512], F32, name="ps") for k in range(size(b) // 4)]
            for g in range(size(b)):
                for hp in range(2):
                    u = 2 * g + hp
                    w0 = (u - (g % 2)) * UNIT
                    v = 2 * goff(b) + u
                    nc.tensor.matmul_mx(
                        out=ps[b][g // 4][:, (g % 4) * 128:(g % 4 + 1) * 128],
                        lhsT=lq[n][:, v * 128:(v + 1) * 128].bitcast(FP8X4),
                        lhsT_scale=ls[n][:, v * 128:(v + 1) * 128],
                        rhs=ck[m][:, w0:w0 + 128].bitcast(FP8X4),
                        rhs_scale=sk[m][:, w0:w0 + 128],
                        start=(hp == 0),
                        stop=(hp == 1),
                    )

        def rowmax(b):
            mx[b] = st_pool.tile([P, G], F32, name="mx")
            for k in range(len(ps[b])):
                nc.vector.tensor_reduce(
                    out=mx[b][:, k * 4:(k + 1) * 4].rearrange("p (a b) -> p a b", a=2, b=2),
                    in_=ps[b][k][:].rearrange("p (a b c) -> p a b c", a=2, b=4, c=64)[:, :, 0:4:3, :],
                    axis=AX.X,
                    op=ALU.max,
                )

        def negmax(b):
            ng = size(b)
            nmx[b] = st_pool.tile([P, G], F32, name="nmx")
            nc.scalar.mul(out=nmx[b][:, 0:ng], in_=mx[b][:, 0:ng], mul=-SCALE)

        def exps(b):
            sm[b] = st_pool.tile([P, G], F32, name="sm")
            et[b] = e_pool.tile([P, G * DH], F32, name="et")
            for g in range(size(b)):
                off = (g % 4) * 128 + (g % 2) * 64
                nc.scalar.activation(
                    out=et[b][:, g * DH:(g + 1) * DH],
                    in_=ps[b][g // 4][:, off:off + DH],
                    func=ACT.Exp,
                    bias=nmx[b][:, g:g + 1],
                    scale=SCALE,
                    accum_out=sm[b][:, g:g + 1],
                )

        def recip(b):
            ng = size(b)
            rs[b] = st_pool.tile([P, G], F32, name="rs")
            nc.vector.reciprocal(out=rs[b][:, 0:ng], in_=sm[b][:, 0:ng])

        def norm_store(b):
            i, g0, g1 = blocks[b]
            ng = g1 - g0
            if b >= nb - NM_V_LAST:
                v = et[b][:, 0:ng * DH].rearrange("p (g c) -> p g c", g=ng, c=DH)
                nc.vector.tensor_tensor(
                    out=v, in0=v, in1=rs[b][:, 0:ng].unsqueeze(2).to_broadcast([P, ng, DH]), op=ALU.mult
                )
            else:
                for g in range(ng):
                    nc.scalar.activation(
                        out=et[b][:, g * DH:(g + 1) * DH],
                        in_=et[b][:, g * DH:(g + 1) * DH],
                        func=ACT.Copy,
                        scale=rs[b][:, g:g + 1],
                    )
            for bb in range(2):
                n0 = (2 * i + bb) * G
                nc.sync.dma_start(
                    out=out[n0 + g0:n0 + g1].rearrange("g a c -> a g c"),
                    in_=et[b][bb * 64:(bb + 1) * 64, 0:ng * DH].rearrange("p (g c) -> p g c", g=ng, c=DH),
                )

        def ok(b):
            return 0 <= b < nb

        ctx.enter_context(tc.manual_schedule())

        zero(0, 0)
        for n in range(NPAIR):
            nc.vector.memset(sq[n][:].bitcast(I32), 0)
        zero(1, 0)
        for i in range(NRAW):
            load(i)
        for it in range(-2, nb + LN + 1):
            if ok(it):
                quant(it, 0)
            if ok(it + 2):
                regroup(it + 2, 1, "s")
            if ok(it - LE):
                negmax(it - LE)
            if ok(it - LN):
                norm_store(it - LN)
            if ok(it - LE):
                exps(it - LE)
            if ok(it):
                quant(it, 1)
            if ok(it + 1):
                regroup(it + 1, 0, "v")
            if ok(it + 2):
                regroup(it + 2, 1, "v")
            if it == -1:
                zero(1, 1)
            if it == 0:
                zero(0, 1)
            if ok(it) and it % 2 == 1:
                moves(it // 2)
                passes(it - 1)
                passes(it)
            if ok(it - LM):
                rowmax(it - LM)
            if ok(it - LR):
                recip(it - LR)
            if ok(it + 1) and last_of_tile[blocks[it + 1][0]] == it + 1 and blocks[it + 1][0] + NRAW < NT:
                load(blocks[it + 1][0] + NRAW)
